import numpy as np
import ml_dtypes


def mxq(x, axis, fmt="e4m3"):
    dtype, down = {"e4m3": (ml_dtypes.float8_e4m3fn, 7), "e5m2": (ml_dtypes.float8_e5m2, 14)}[fmt]
    v = np.moveaxis(np.asarray(x, np.float32).astype(ml_dtypes.bfloat16).astype(np.float64), axis, -1)
    blocks = v.reshape(v.shape[:-1] + (-1, 32))
    amax = np.abs(blocks).max(-1, keepdims=True)
    byte = np.maximum(np.where(amax > 0, np.frexp(amax)[1] - 1 + 127, 0) - down, 1)
    scale = np.exp2(byte - 127.0)
    codes = (blocks / scale).astype(np.float32).astype(dtype).astype(np.float64)
    return np.moveaxis((codes * scale).reshape(v.shape), -1, axis)


WIDE = False


def mx_kscale(k):
    if not WIDE:
        return np.ones(k)
    levels = np.array([10, -10, 5, -5, 0])
    a = np.random.permutation(np.resize(levels, k // 512 * 4)).reshape(k // 512, 4)
    idx = np.arange(k)
    return np.exp2(a[idx // 512, idx % 128 // 32])


BF16 = ml_dtypes.bfloat16


def bf(x):
    return np.asarray(x, np.float32).astype(BF16)


def f64(x):
    return np.asarray(x).astype(np.float64)


N, D_FEAT, D_EMB, H = 4, 511, 512, 4
SEQ = D_FEAT + 1
EPS = 1e-5


def ln(x):
    m = x.mean(-1, keepdims=True)
    v = ((x - m) ** 2).mean(-1, keepdims=True)
    return (x - m) / np.sqrt(v + EPS)


def setup_inputs():
    s = mx_kscale(D_EMB)
    return {'Z': bf(0.5 + 1.5 * np.random.standard_normal((N, D_FEAT))),
            'feat_emb': bf(np.random.standard_normal((D_FEAT, D_EMB)) * 0.02 + 0.01),
            'label_token': bf(np.random.standard_normal((1, 1, D_EMB)) * 0.02 + 0.01),
            'g1': bf((1.0 + 0.1 * np.random.standard_normal(D_EMB)) * s),
            'be1': bf(0.1 * np.random.standard_normal(D_EMB) * s),
            'wk': bf(np.random.standard_normal((D_EMB, D_EMB)) / np.sqrt(D_EMB) / s[:, None]),
            'bk': bf(0.3 * np.random.standard_normal(D_EMB)),
            'wv': bf(np.random.standard_normal((D_EMB, D_EMB)) / np.sqrt(D_EMB) / s[:, None]),
            'bv': bf(0.3 * np.random.standard_normal(D_EMB))}


def reference(Z, feat_emb, label_token, g1, be1, wk, bk, wv, bv):
    n = Z.shape[0]
    zn = ln(f64(Z))
    x_feats = zn[..., None] * f64(feat_emb)[None]
    lab = np.broadcast_to(f64(label_token), (n, 1, D_EMB))
    x = np.concatenate([x_feats, lab], axis=1)
    xn = ln(x) * f64(g1) + f64(be1)
    xq = mxq(xn, 2, 'e4m3')
    k = (xq @ mxq(f64(wk), 0, 'e4m3')) + f64(bk)
    v = (xq @ mxq(f64(wv), 0, 'e4m3')) + f64(bv)
    return k, v

@@ -1,0 +1,236 @@
+from contextlib import ExitStack
+
+import concourse.mybir as mybir
+from concourse.masks import make_identity
+
+F32 = mybir.dt.float32
+BF16 = mybir.dt.bfloat16
+U32 = mybir.dt.uint32
+U8 = mybir.dt.uint8
+FP8X4 = mybir.dt.float8_e4m3fn_x4
+ALU = mybir.AluOpType
+ACT = mybir.ActivationFunctionType
+
+P = 128
+PACK = 4
+BATCH = 4
+D_FEAT = 511
+SEQ = D_FEAT + 1
+D_EMB = 512
+D_OUT = 512
+BLOCKS = SEQ // P
+EPS = 1e-5
+
+FLOPS = 2 * BATCH * SEQ * D_EMB * 2 * D_OUT
+
+
+def tile_causalfeaturetransformer_pa_kernel(
+    tc, Z, feat_emb, label_token, g1, be1, wk, bk, wv, bv, out_0, out_1
+):
+    nc = tc.nc
+    weights = (wk, wv)
+    outs = (out_0, out_1)
+
+    with ExitStack() as ctx:
+        keep = ctx.enter_context(tc.tile_pool(name="keep", bufs=1))
+        stage = ctx.enter_context(tc.tile_pool(name="stage", bufs=3))
+        result_pool = ctx.enter_context(tc.tile_pool(name="result", bufs=6))
+        setup_bank = ctx.enter_context(tc.psum_pool(name="setup_bank", bufs=1))
+        turned_banks = ctx.enter_context(tc.psum_pool(name="turned_banks", bufs=3))
+        acc_banks = ctx.enter_context(tc.psum_pool(name="acc_banks", bufs=4))
+        ctx.enter_context(tc.manual_schedule())
+
+        ident = keep.tile([P, P], F32)
+        ident_bf = keep.tile([P, P], BF16)
+        warm = keep.tile([P, 1], F32)
+        z_rows = keep.tile([P, SEQ], BF16)
+        vec_rows = keep.tile([P, SEQ], BF16)
+        emb = keep.tile([P, BLOCKS, D_EMB], BF16)
+        z_stats = keep.tile([P, 6], F32)
+        z_mv = keep.tile([P, 2], F32)
+        z_rstd = keep.tile([P, 1], F32)
+        zn = keep.tile([P, SEQ], F32)
+        factor = keep.tile([P, BLOCKS, BATCH], F32)
+        e_stats = keep.tile([P, BLOCKS, 6], F32)
+        e_mv = keep.tile([P, BLOCKS, 2], F32)
+        shaped = keep.tile([P, BLOCKS, D_EMB], F32)
+        slope = keep.tile([P, BLOCKS, BATCH], F32)
+        spread = [keep.tile([P, SEQ], BF16, name="spread%d" % r) for r in range(4)]
+        g1_all, be1_all = spread[0], spread[1]
+        w_raw = [keep.tile([P, PACK, D_OUT], BF16, name="w_raw%d" % w) for w in range(2)]
+        w_grouped = [
+            keep.tile([P, D_OUT, PACK], BF16, name="w_grouped%d" % w, align_bytes=64) for w in range(2)
+        ]
+        w_codes = [keep.tile([P, D_OUT], U32, name="w_codes%d" % w, align_bytes=64) for w in range(2)]
+        w_scales = [keep.tile([P, D_OUT], U8, name="w_scales%d" % w, align_bytes=64) for w in range(2)]
+
+        def spread_vector(r):
+            bank = acc_banks.tile([P, SEQ], F32, name="acc")
+            nc.tensor.matmul(
+                out=bank[:],
+                lhsT=ident_bf[:, r : r + 1].to_broadcast([P, P]),
+                rhs=vec_rows[:],
+                start=True,
+                stop=True,
+            )
+            nc.scalar.copy(out=spread[r][:], in_=bank[:])
+
+        def measure(j):
+            nc.vector.bn_stats(out=e_stats[:, j, :], in_=emb[:, j, :])
+            nc.vector.bn_aggr(out=e_mv[:, j, :], in_=e_stats[:, j, :])
+
+        def shape(j):
+            nc.vector.scalar_tensor_tensor(
+                out=shaped[:, j, :],
+                in0=emb[:, j, :],
+                scalar=e_mv[:, j, 0:1],
+                in1=g1_all[:],
+                op0=ALU.subtract,
+                op1=ALU.mult,
+            )
+
+        def slope_root(j):
+            nc.vector.tensor_mul(out=slope[:, j, :], in0=factor[:, j, :], in1=factor[:, j, :])
+            nc.vector.tensor_scalar(
+                out=slope[:, j, :],
+                in0=slope[:, j, :],
+                scalar1=e_mv[:, j, 1:2],
+                scalar2=EPS,
+                op0=ALU.mult,
+                op1=ALU.add,
+            )
+            nc.scalar.activation(out=slope[:, j, :], in_=slope[:, j, :], func=ACT.Sqrt)
+
+        def slope_divide(j):
+            nc.vector.reciprocal(out=slope[:, j, :], in_=slope[:, j, :])
+            nc.vector.tensor_mul(out=slope[:, j, :], in0=slope[:, j, :], in1=factor[:, j, :])
+
+        def regroup_weight(w):
+            nc.vector.tensor_copy(
+                out=w_grouped[w][:].rearrange("p (c i) t -> p c t i", i=4),
+                in_=w_raw[w][:].rearrange("p t (c i) -> p c t i", i=4),
+            )
+
+        def quantise_weight(w):
+            nc.vector.quantize_mx(
+                out=w_codes[w][:].bitcast(FP8X4),
+                scales=w_scales[w][:],
+                in_=w_grouped[w][:].rearrange("p n t -> p (n t)"),
+            )
+
+        nc.sync.dma_start(out=z_rows[0:BATCH, 0:D_FEAT], in_=Z)
+        nc.sync.dma_start(out=emb[:, 0, :], in_=feat_emb[0:P, :])
+        nc.vector.memset(vec_rows[:], 0.0)
+        vectors = (g1, be1, bk, bv)
+        for r in range(4):
+            nc.sync.dma_start(out=vec_rows[r : r + 1, :], in_=vectors[r].rearrange("(a k) -> a k", a=1))
+        for w in range(2):
+            nc.sync.dma_start(out=w_raw[w][:], in_=weights[w].rearrange("(t p) n -> p t n", p=P))
+        for j in range(1, BLOCKS - 1):
+            nc.sync.dma_start(out=emb[:, j, :], in_=feat_emb[j * P : (j + 1) * P, :])
+        last = (BLOCKS - 1) * P
+        nc.sync.dma_start(out=emb[0:112, BLOCKS - 1, :], in_=feat_emb[last : last + 112, :])
+        nc.sync.dma_start(out=emb[112:127, BLOCKS - 1, :], in_=feat_emb[last + 112 : D_FEAT, :])
+        nc.sync.dma_start(
+            out=emb[127:128, BLOCKS - 1, :], in_=label_token.rearrange("a b k -> (a b) k")
+        )
+
+        make_identity(nc, ident[:])
+        nc.vector.memset(warm[:], 1.0)
+        nc.scalar.activation(out=warm[:], in_=warm[:], func=ACT.Sqrt)
+        nc.vector.memset(zn[:], 0.0)
+        nc.vector.memset(zn[0:BATCH, D_FEAT:SEQ], 1.0)
+        nc.vector.tensor_copy(out=ident_bf[:], in_=ident[:])
+
+        rows4 = slice(0, BATCH)
+        nc.vector.bn_stats(out=z_stats[rows4, :], in_=z_rows[rows4, 0:D_FEAT])
+        nc.vector.bn_aggr(out=z_mv[rows4, :], in_=z_stats[rows4, :])
+        nc.vector.tensor_scalar_add(out=z_rstd[rows4, :], in0=z_mv[rows4, 1:2], scalar1=EPS)
+        nc.scalar.activation(out=z_rstd[rows4, :], in_=z_rstd[rows4, :], func=ACT.Sqrt)
+        measure(0)
+        nc.vector.reciprocal(out=z_rstd[rows4, :], in_=z_rstd[rows4, :])
+        nc.vector.tensor_scalar(
+            out=zn[rows4, 0:D_FEAT],
+            in0=z_rows[rows4, 0:D_FEAT],
+            scalar1=z_mv[rows4, 0:1],
+            scalar2=z_rstd[rows4, 0:1],
+            op0=ALU.subtract,
+            op1=ALU.mult,
+        )
+        spread_vector(0)
+        spread_vector(1)
+        zn_turned = setup_bank.tile([P, BLOCKS, P], F32)
+        for j in range(BLOCKS):
+            nc.tensor.transpose(zn_turned[:, j, :], zn[:, j * P : (j + 1) * P], ident[:])
+        shape(0)
+        nc.vector.tensor_copy(out=factor[:], in_=zn_turned[:, :, 0:BATCH])
+        slope_root(0)
+        regroup_weight(0)
+        slope_divide(0)
+        regroup_weight(1)
+        quantise_weight(0)
+        quantise_weight(1)
+
+        scaled, xn, turned, x_grouped, x_codes, x_scales = {}, {}, {}, {}, {}, {}
+
+        def scale_and_shift(u):
+            j, n = divmod(u, BATCH)
+            scaled[u] = stage.tile([P, D_EMB], F32, name="scaled")
+            nc.scalar.activation(
+                out=scaled[u][:], in_=shaped[:, j, :], func=ACT.Copy, scale=slope[:, j, n : n + 1]
+            )
+            xn[u] = stage.tile([P, D_EMB], BF16, name="xn")
+            nc.gpsimd.tensor_tensor(out=xn[u][:], in0=scaled[u][:], in1=be1_all[:], op=ALU.add)
+
+        def turn(u):
+            turned[u] = turned_banks.tile([P, PACK, P], BF16, name="turned")
+            for t in range(PACK):
+                nc.tensor.transpose(turned[u][:, t, :], xn[u][:, t * P : (t + 1) * P], ident_bf[:])
+
+        def regroup_and_quantise(u):
+            x_grouped[u] = stage.tile([P, P, PACK], BF16, name="x_grouped", align_bytes=64)
+            nc.scalar.copy(out=x_grouped[u][:], in_=turned[u][:].rearrange("p t r -> p r t"))
+            x_codes[u] = stage.tile([P, P], U32, name="x_codes", align_bytes=64)
+            x_scales[u] = stage.tile([P, P], U8, name="x_scales", align_bytes=64)
+            nc.vector.quantize_mx(
+                out=x_codes[u][:].bitcast(FP8X4),
+                scales=x_scales[u][:],
+                in_=x_grouped[u][:].rearrange("p r t -> p (r t)"),
+            )
+
+        def multiply_and_store(u):
+            j, n = divmod(u, BATCH)
+            for w in range(2):
+                acc = acc_banks.tile([P, D_OUT], F32)
+                nc.tensor.matmul_mx(
+                    out=acc[:],
+                    lhsT=x_codes[u][:].bitcast(FP8X4),
+                    lhsT_scale=x_scales[u][:],
+                    rhs=w_codes[w][:].bitcast(FP8X4),
+                    rhs_scale=w_scales[w][:],
+                    start=True,
+                    stop=True,
+                )
+                result = result_pool.tile([P, D_OUT], F32)
+                nc.vector.tensor_add(out=result[:], in0=acc[:], in1=spread[2 + w][:])
+                nc.sync.dma_start(out=outs[w][n, j * P : (j + 1) * P, :], in_=result[:])
+
+        units = BLOCKS * BATCH
+        for step in range(units + 3):
+            if step < units:
+                scale_and_shift(step)
+            if step < 2:
+                spread_vector(2 + step)
+            if 1 <= step <= units:
+                turn(step - 1)
+            if 2 <= step <= units + 1:
+                regroup_and_quantise(step - 2)
+            if 3 <= step:
+                multiply_and_store(step - 3)
+            next_block = step // BATCH + 1
+            if next_block < BLOCKS and step % BATCH == 0:
+                measure(next_block)
+                shape(next_block)
+                slope_root(next_block)
+            if next_block < BLOCKS and step % BATCH == 1:
+                slope_divide(next_block)

@@ -21,6 +21,13 @@ D_OUT = 512
 BLOCKS = SEQ // P
 EPS = 1e-5
 
+UNITS = BLOCKS * BATCH
+PAIR = 2
+PAIRS = UNITS // PAIR
+VECTOR_UNITS = BATCH
+TURN_AHEAD = 2
+FORM_AHEAD = 4
+
 FLOPS = 2 * BATCH * SEQ * D_EMB * 2 * D_OUT
 
 
@@ -33,29 +40,27 @@ def tile_causalfeaturetransformer_pa_kernel(
 
     with ExitStack() as ctx:
         keep = ctx.enter_context(tc.tile_pool(name="keep", bufs=1))
-        stage = ctx.enter_context(tc.tile_pool(name="stage", bufs=3))
-        result_pool = ctx.enter_context(tc.tile_pool(name="result", bufs=6))
-        setup_bank = ctx.enter_context(tc.psum_pool(name="setup_bank", bufs=1))
-        turned_banks = ctx.enter_context(tc.psum_pool(name="turned_banks", bufs=3))
-        acc_banks = ctx.enter_context(tc.psum_pool(name="acc_banks", bufs=4))
+        turned_banks = ctx.enter_context(tc.psum_pool(name="turned_banks", bufs=2))
+        acc_banks = ctx.enter_context(tc.psum_pool(name="acc_banks", bufs=6))
         ctx.enter_context(tc.manual_schedule())
 
         ident = keep.tile([P, P], F32)
         ident_bf = keep.tile([P, P], BF16)
         warm = keep.tile([P, 1], F32)
         z_rows = keep.tile([P, SEQ], BF16)
-        vec_rows = keep.tile([P, SEQ], BF16)
+        vec_rows = keep.tile([P, D_EMB], BF16)
         emb = keep.tile([P, BLOCKS, D_EMB], BF16)
         z_stats = keep.tile([P, 6], F32)
         z_mv = keep.tile([P, 2], F32)
-        z_rstd = keep.tile([P, 1], F32)
-        zn = keep.tile([P, SEQ], F32)
-        factor = keep.tile([P, BLOCKS, BATCH], F32)
+        z_var_eps = keep.tile([P, 1], F32)
+        z_terms = keep.tile([P, P + SEQ], F32)
+        z_turned = keep.tile([P, 1 + BLOCKS, BATCH], F32)
         e_stats = keep.tile([P, BLOCKS, 6], F32)
         e_mv = keep.tile([P, BLOCKS, 2], F32)
         shaped = keep.tile([P, BLOCKS, D_EMB], F32)
+        root = keep.tile([P, BLOCKS, 2 * BATCH], F32)
         slope = keep.tile([P, BLOCKS, BATCH], F32)
-        spread = [keep.tile([P, SEQ], BF16, name="spread%d" % r) for r in range(4)]
+        spread = [keep.tile([P, D_EMB], BF16, name="spread%d" % r) for r in range(4)]
         g1_all, be1_all = spread[0], spread[1]
         w_raw = [keep.tile([P, PACK, D_OUT], BF16, name="w_raw%d" % w) for w in range(2)]
         w_grouped = [
@@ -63,9 +68,18 @@ def tile_causalfeaturetransformer_pa_kernel(
         ]
         w_codes = [keep.tile([P, D_OUT], U32, name="w_codes%d" % w, align_bytes=64) for w in range(2)]
         w_scales = [keep.tile([P, D_OUT], U8, name="w_scales%d" % w, align_bytes=64) for w in range(2)]
+        scaled = {u: keep.tile([P, D_EMB], F32, name="scaled%d" % u) for u in range(VECTOR_UNITS, UNITS)}
+        xn = [keep.tile([P, D_EMB], BF16, name="xn%d" % u) for u in range(UNITS)]
+        x_grouped = [
+            keep.tile([P, PAIR, P, PACK], BF16, name="x_grouped%d" % c, align_bytes=64)
+            for c in range(PAIRS)
+        ]
+        x_codes = [keep.tile([P, PAIR * P], U32, name="x_codes%d" % c, align_bytes=64) for c in range(PAIRS)]
+        x_scales = [keep.tile([P, PAIR * P], U8, name="x_scales%d" % c, align_bytes=64) for c in range(PAIRS)]
+        result = [keep.tile([P, D_OUT], F32, name="result%d" % b) for b in range(2 * UNITS)]
 
         def spread_vector(r):
-            bank = acc_banks.tile([P, SEQ], F32, name="acc")
+            bank = acc_banks.tile([P, D_EMB], F32, name="acc")
             nc.tensor.matmul(
                 out=bank[:],
                 lhsT=ident_bf[:, r : r + 1].to_broadcast([P, P]),
@@ -74,6 +88,12 @@ def tile_causalfeaturetransformer_pa_kernel(
                 stop=True,
             )
             nc.scalar.copy(out=spread[r][:], in_=bank[:])
+
+        def turn_z_terms(first, end):
+            bank = turned_banks.tile([P, BLOCKS, P], F32, name="turned")
+            for b in range(first, end):
+                nc.tensor.transpose(bank[:, b - first, :], z_terms[:, b * P : (b + 1) * P], ident[:])
+            nc.vector.tensor_copy(out=z_turned[:, first:end, :], in_=bank[:, 0 : end - first, 0:BATCH])
 
         def measure(j):
             nc.vector.bn_stats(out=e_stats[:, j, :], in_=emb[:, j, :])
@@ -89,26 +109,20 @@ def tile_causalfeaturetransformer_pa_kernel(
                 op1=ALU.mult,
             )
 
-        def slope_root(j):
-            nc.vector.tensor_mul(out=slope[:, j, :], in0=factor[:, j, :], in1=factor[:, j, :])
-            nc.vector.tensor_scalar(
-                out=slope[:, j, :],
-                in0=slope[:, j, :],
-                scalar1=e_mv[:, j, 1:2],
-                scalar2=EPS,
-                op0=ALU.mult,
-                op1=ALU.add,
-            )
-            nc.scalar.activation(out=slope[:, j, :], in_=slope[:, j, :], func=ACT.Sqrt)
+        def slope_root(first, end):
+            d = z_turned[:, 1 + first : 1 + end, :]
+            part = root[:, first:end, 0:BATCH]
+            some = [P, end - first, BATCH]
+            nc.vector.tensor_mul(out=part, in0=d, in1=d)
+            nc.vector.tensor_mul(out=part, in0=part, in1=e_mv[:, first:end, 1:2].to_broadcast(some))
+            nc.vector.tensor_add(out=part, in0=part, in1=z_turned[:, 0:1, :].to_broadcast(some))
+            nc.scalar.activation(out=part, in_=part, func=ACT.Sqrt)
 
-        def slope_divide(j):
-            nc.vector.reciprocal(out=slope[:, j, :], in_=slope[:, j, :])
-            nc.vector.tensor_mul(out=slope[:, j, :], in0=slope[:, j, :], in1=factor[:, j, :])
-
-        def regroup_weight(w):
-            nc.vector.tensor_copy(
-                out=w_grouped[w][:].rearrange("p (c i) t -> p c t i", i=4),
-                in_=w_raw[w][:].rearrange("p t (c i) -> p c t i", i=4),
+        def slope_divide(first, end):
+            part = root[:, first:end, 0:BATCH]
+            nc.vector.reciprocal(out=part, in_=part)
+            nc.vector.tensor_mul(
+                out=slope[:, first:end, :], in0=part, in1=z_turned[:, 1 + first : 1 + end, :]
             )
 
         def quantise_weight(w):
@@ -118,16 +132,83 @@ def tile_causalfeaturetransformer_pa_kernel(
                 in_=w_grouped[w][:].rearrange("p n t -> p (n t)"),
             )
 
+        def form_on_vector(u):
+            j, n = divmod(u, BATCH)
+            nc.vector.scalar_tensor_tensor(
+                out=xn[u][:],
+                in0=shaped[:, j, :],
+                scalar=slope[:, j, n : n + 1],
+                in1=be1_all[:],
+                op0=ALU.mult,
+                op1=ALU.add,
+            )
+
+        def form_on_scalar_and_gpsimd(u):
+            j, n = divmod(u, BATCH)
+            nc.scalar.activation(
+                out=scaled[u][:], in_=shaped[:, j, :], func=ACT.Copy, scale=slope[:, j, n : n + 1]
+            )
+            nc.gpsimd.tensor_tensor(out=xn[u][:], in0=scaled[u][:], in1=be1_all[:], op=ALU.add)
+
+        def turn_and_regroup(c):
+            turned = turned_banks.tile([P, PAIR, PACK, P], BF16)
+            for h in range(PAIR):
+                for t in range(PACK):
+                    nc.tensor.transpose(
+                        turned[:, h, t, :], xn[PAIR * c + h][:, t * P : (t + 1) * P], ident_bf[:]
+                    )
+            nc.scalar.copy(out=x_grouped[c][:], in_=turned[:].rearrange("p h t r -> p h r t"))
+
+        def quantise(c):
+            nc.vector.quantize_mx(
+                out=x_codes[c][:].bitcast(FP8X4),
+                scales=x_scales[c][:],
+                in_=x_grouped[c][:].rearrange("p h r t -> p (h r t)"),
+            )
+
+        def multiply(c):
+            banks = []
+            for h in range(PAIR):
+                tokens = slice(h * P, (h + 1) * P)
+                for w in range(2):
+                    acc = acc_banks.tile([P, D_OUT], F32)
+                    nc.tensor.matmul_mx(
+                        out=acc[:],
+                        lhsT=x_codes[c][:, tokens].bitcast(FP8X4),
+                        lhsT_scale=x_scales[c][:, tokens],
+                        rhs=w_codes[w][:].bitcast(FP8X4),
+                        rhs_scale=w_scales[w][:],
+                        start=True,
+                        stop=True,
+                    )
+                    banks.append(acc)
+            return banks
+
+        def add_bias_and_store(c, h, banks):
+            j, n = divmod(PAIR * c + h, BATCH)
+            for w in range(2):
+                b = 2 * h + w
+                res = result[2 * PAIR * c + b]
+                nc.vector.tensor_add(out=res[:], in0=banks[b][:], in1=spread[2 + w][:])
+                nc.sync.dma_start(out=outs[w][n, j * P : (j + 1) * P, :], in_=res[:])
+
+        def load_vector(r, vector):
+            nc.sync.dma_start(out=vec_rows[r : r + 1, :], in_=vector.rearrange("(a k) -> a k", a=1))
+
+        def load_weight(w):
+            nc.sync.dma_start(out=w_raw[w][:], in_=weights[w].rearrange("(t p) n -> p t n", p=P))
+
+        nc.vector.memset(vec_rows[:], 0.0)
         nc.sync.dma_start(out=z_rows[0:BATCH, 0:D_FEAT], in_=Z)
         nc.sync.dma_start(out=emb[:, 0, :], in_=feat_emb[0:P, :])
-        nc.vector.memset(vec_rows[:], 0.0)
-        vectors = (g1, be1, bk, bv)
-        for r in range(4):
-            nc.sync.dma_start(out=vec_rows[r : r + 1, :], in_=vectors[r].rearrange("(a k) -> a k", a=1))
-        for w in range(2):
-            nc.sync.dma_start(out=w_raw[w][:], in_=weights[w].rearrange("(t p) n -> p t n", p=P))
-        for j in range(1, BLOCKS - 1):
-            nc.sync.dma_start(out=emb[:, j, :], in_=feat_emb[j * P : (j + 1) * P, :])
+        load_vector(0, g1)
+        load_vector(1, be1)
+        load_vector(2, bk)
+        load_vector(3, bv)
+        nc.sync.dma_start(out=emb[:, 1, :], in_=feat_emb[P : 2 * P, :])
+        load_weight(0)
+        load_weight(1)
+        nc.sync.dma_start(out=emb[:, 2, :], in_=feat_emb[2 * P : 3 * P, :])
         last = (BLOCKS - 1) * P
         nc.sync.dma_start(out=emb[0:112, BLOCKS - 1, :], in_=feat_emb[last : last + 112, :])
         nc.sync.dma_start(out=emb[112:127, BLOCKS - 1, :], in_=feat_emb[last + 112 : D_FEAT, :])
@@ -136,101 +217,78 @@ def tile_causalfeaturetransformer_pa_kernel(
         )
 
         make_identity(nc, ident[:])
+        nc.gpsimd.memset(z_terms[:], 0.0)
         nc.vector.memset(warm[:], 1.0)
         nc.scalar.activation(out=warm[:], in_=warm[:], func=ACT.Sqrt)
-        nc.vector.memset(zn[:], 0.0)
-        nc.vector.memset(zn[0:BATCH, D_FEAT:SEQ], 1.0)
         nc.vector.tensor_copy(out=ident_bf[:], in_=ident[:])
 
         rows4 = slice(0, BATCH)
         nc.vector.bn_stats(out=z_stats[rows4, :], in_=z_rows[rows4, 0:D_FEAT])
         nc.vector.bn_aggr(out=z_mv[rows4, :], in_=z_stats[rows4, :])
-        nc.vector.tensor_scalar_add(out=z_rstd[rows4, :], in0=z_mv[rows4, 1:2], scalar1=EPS)
-        nc.scalar.activation(out=z_rstd[rows4, :], in_=z_rstd[rows4, :], func=ACT.Sqrt)
-        measure(0)
-        nc.vector.reciprocal(out=z_rstd[rows4, :], in_=z_rstd[rows4, :])
+        nc.vector.tensor_scalar_sub(
+            out=z_terms[rows4, P : P + D_FEAT], in0=z_rows[rows4, 0:D_FEAT], scalar1=z_mv[rows4, 0:1]
+        )
         nc.vector.tensor_scalar(
-            out=zn[rows4, 0:D_FEAT],
-            in0=z_rows[rows4, 0:D_FEAT],
-            scalar1=z_mv[rows4, 0:1],
-            scalar2=z_rstd[rows4, 0:1],
-            op0=ALU.subtract,
+            out=z_terms[rows4, 0:P],
+            in0=z_mv[rows4, 1:2].to_broadcast([BATCH, P]),
+            scalar1=EPS,
+            scalar2=EPS,
+            op0=ALU.add,
             op1=ALU.mult,
         )
+        nc.vector.tensor_scalar_add(out=z_var_eps[rows4, :], in0=z_mv[rows4, 1:2], scalar1=EPS)
         spread_vector(0)
         spread_vector(1)
-        zn_turned = setup_bank.tile([P, BLOCKS, P], F32)
-        for j in range(BLOCKS):
-            nc.tensor.transpose(zn_turned[:, j, :], zn[:, j * P : (j + 1) * P], ident[:])
+        nc.scalar.activation(
+            out=z_terms[rows4, P + D_FEAT : P + SEQ], in_=z_var_eps[rows4, :], func=ACT.Sqrt
+        )
+        measure(0)
         shape(0)
-        nc.vector.tensor_copy(out=factor[:], in_=zn_turned[:, :, 0:BATCH])
-        slope_root(0)
-        regroup_weight(0)
-        slope_divide(0)
-        regroup_weight(1)
+        turn_z_terms(0, 2)
+        slope_root(0, 1)
+        measure(1)
+        slope_divide(0, 1)
+        spread_vector(2)
+        spread_vector(3)
+        nc.scalar.copy(out=w_grouped[0][:], in_=w_raw[0][:].rearrange("p t n -> p n t"))
+        nc.gpsimd.tensor_scalar(
+            out=w_grouped[1][:],
+            in0=w_raw[1][:].rearrange("p t n -> p n t"),
+            scalar1=1.0,
+            scalar2=0.0,
+            op0=ALU.mult,
+            op1=ALU.add,
+        )
+        form_on_vector(0)
+        form_on_vector(1)
+        turn_z_terms(2, 1 + BLOCKS)
+        measure(2)
+        measure(3)
+        slope_root(1, BLOCKS)
+        shape(1)
+        slope_divide(1, BLOCKS)
+        form_on_scalar_and_gpsimd(4)
+        form_on_scalar_and_gpsimd(5)
+        turn_and_regroup(0)
+        form_on_vector(2)
+        form_on_vector(3)
+        form_on_scalar_and_gpsimd(6)
+        form_on_scalar_and_gpsimd(7)
+        turn_and_regroup(1)
         quantise_weight(0)
         quantise_weight(1)
+        shape(2)
+        quantise(0)
+        shape(3)
 
-        scaled, xn, turned, x_grouped, x_codes, x_scales = {}, {}, {}, {}, {}, {}
-
-        def scale_and_shift(u):
-            j, n = divmod(u, BATCH)
-            scaled[u] = stage.tile([P, D_EMB], F32, name="scaled")
-            nc.scalar.activation(
-                out=scaled[u][:], in_=shaped[:, j, :], func=ACT.Copy, scale=slope[:, j, n : n + 1]
-            )
-            xn[u] = stage.tile([P, D_EMB], BF16, name="xn")
-            nc.gpsimd.tensor_tensor(out=xn[u][:], in0=scaled[u][:], in1=be1_all[:], op=ALU.add)
-
-        def turn(u):
-            turned[u] = turned_banks.tile([P, PACK, P], BF16, name="turned")
-            for t in range(PACK):
-                nc.tensor.transpose(turned[u][:, t, :], xn[u][:, t * P : (t + 1) * P], ident_bf[:])
-
-        def regroup_and_quantise(u):
-            x_grouped[u] = stage.tile([P, P, PACK], BF16, name="x_grouped", align_bytes=64)
-            nc.scalar.copy(out=x_grouped[u][:], in_=turned[u][:].rearrange("p t r -> p r t"))
-            x_codes[u] = stage.tile([P, P], U32, name="x_codes", align_bytes=64)
-            x_scales[u] = stage.tile([P, P], U8, name="x_scales", align_bytes=64)
-            nc.vector.quantize_mx(
-                out=x_codes[u][:].bitcast(FP8X4),
-                scales=x_scales[u][:],
-                in_=x_grouped[u][:].rearrange("p r t -> p (r t)"),
-            )
-
-        def multiply_and_store(u):
-            j, n = divmod(u, BATCH)
-            for w in range(2):
-                acc = acc_banks.tile([P, D_OUT], F32)
-                nc.tensor.matmul_mx(
-                    out=acc[:],
-                    lhsT=x_codes[u][:].bitcast(FP8X4),
-                    lhsT_scale=x_scales[u][:],
-                    rhs=w_codes[w][:].bitcast(FP8X4),
-                    rhs_scale=w_scales[w][:],
-                    start=True,
-                    stop=True,
-                )
-                result = result_pool.tile([P, D_OUT], F32)
-                nc.vector.tensor_add(out=result[:], in0=acc[:], in1=spread[2 + w][:])
-                nc.sync.dma_start(out=outs[w][n, j * P : (j + 1) * P, :], in_=result[:])
-
-        units = BLOCKS * BATCH
-        for step in range(units + 3):
-            if step < units:
-                scale_and_shift(step)
-            if step < 2:
-                spread_vector(2 + step)
-            if 1 <= step <= units:
-                turn(step - 1)
-            if 2 <= step <= units + 1:
-                regroup_and_quantise(step - 2)
-            if 3 <= step:
-                multiply_and_store(step - 3)
-            next_block = step // BATCH + 1
-            if next_block < BLOCKS and step % BATCH == 0:
-                measure(next_block)
-                shape(next_block)
-                slope_root(next_block)
-            if next_block < BLOCKS and step % BATCH == 1:
-                slope_divide(next_block)
+        for step in range(PAIRS):
+            banks = multiply(step)
+            if step + FORM_AHEAD < PAIRS:
+                for h in range(PAIR):
+                    form_on_scalar_and_gpsimd(PAIR * (step + FORM_AHEAD) + h)
+            if step + TURN_AHEAD < PAIRS:
+                turn_and_regroup(step + TURN_AHEAD)
+            add_bias_and_store(step, 0, banks)
+            if step + 1 < PAIRS:
+                quantise(step + 1)
+            add_bias_and_store(step, 1, banks)

@@ -24,6 +24,7 @@ EPS = 1e-5
 UNITS = BLOCKS * BATCH
 PAIR = 2
 PAIRS = UNITS // PAIR
+PAIR_BANKS = 2 * PAIR
 VECTOR_UNITS = BATCH
 TURN_AHEAD = 2
 FORM_AHEAD = 4
@@ -48,20 +49,20 @@ def tile_causalfeaturetransformer_pa_kernel(
         ident_bf = keep.tile([P, P], BF16)
         warm = keep.tile([P, 1], F32)
         z_rows = keep.tile([P, SEQ], BF16)
-        vec_rows = keep.tile([P, D_EMB], BF16)
+        norm_rows = keep.tile([P, D_EMB], BF16)
+        bias_rows = keep.tile([P, D_OUT], BF16)
         emb = keep.tile([P, BLOCKS, D_EMB], BF16)
         z_stats = keep.tile([P, 6], F32)
         z_mv = keep.tile([P, 2], F32)
         z_var_eps = keep.tile([P, 1], F32)
         z_terms = keep.tile([P, P + SEQ], F32)
-        z_turned = keep.tile([P, 1 + BLOCKS, BATCH], F32)
         e_stats = keep.tile([P, BLOCKS, 6], F32)
         e_mv = keep.tile([P, BLOCKS, 2], F32)
         shaped = keep.tile([P, BLOCKS, D_EMB], F32)
         root = keep.tile([P, BLOCKS, 2 * BATCH], F32)
         slope = keep.tile([P, BLOCKS, BATCH], F32)
-        spread = [keep.tile([P, D_EMB], BF16, name="spread%d" % r) for r in range(4)]
-        g1_all, be1_all = spread[0], spread[1]
+        be1_all = keep.tile([P, D_EMB], BF16)
+        bias_all = [keep.tile([P, D_OUT], BF16, name="bias_all%d" % w) for w in range(2)]
         w_raw = [keep.tile([P, PACK, D_OUT], BF16, name="w_raw%d" % w) for w in range(2)]
         w_grouped = [
             keep.tile([P, D_OUT, PACK], BF16, name="w_grouped%d" % w, align_bytes=64) for w in range(2)
@@ -78,22 +79,23 @@ def tile_causalfeaturetransformer_pa_kernel(
         x_scales = [keep.tile([P, PAIR * P], U8, name="x_scales%d" % c, align_bytes=64) for c in range(PAIRS)]
         result = [keep.tile([P, D_OUT], F32, name="result%d" % b) for b in range(2 * UNITS)]
 
-        def spread_vector(r):
+        def spread_row(rows, r):
             bank = acc_banks.tile([P, D_EMB], F32, name="acc")
             nc.tensor.matmul(
                 out=bank[:],
                 lhsT=ident_bf[:, r : r + 1].to_broadcast([P, P]),
-                rhs=vec_rows[:],
+                rhs=rows[:],
                 start=True,
                 stop=True,
             )
-            nc.scalar.copy(out=spread[r][:], in_=bank[:])
+            return bank
 
         def turn_z_terms(first, end):
             bank = turned_banks.tile([P, BLOCKS, P], F32, name="turned")
-            for b in range(first, end):
-                nc.tensor.transpose(bank[:, b - first, :], z_terms[:, b * P : (b + 1) * P], ident[:])
-            nc.vector.tensor_copy(out=z_turned[:, first:end, :], in_=bank[:, 0 : end - first, 0:BATCH])
+            nc.tensor.transpose(bank[:, 0, :], z_terms[:, 0:P], ident[:])
+            for j in range(first, end):
+                nc.tensor.transpose(bank[:, 1 + j - first, :], z_terms[:, (1 + j) * P : (2 + j) * P], ident[:])
+            return bank
 
         def measure(j):
             nc.vector.bn_stats(out=e_stats[:, j, :], in_=emb[:, j, :])
@@ -104,25 +106,33 @@ def tile_causalfeaturetransformer_pa_kernel(
                 out=shaped[:, j, :],
                 in0=emb[:, j, :],
                 scalar=e_mv[:, j, 0:1],
-                in1=g1_all[:],
+                in1=g1_bank[:],
                 op0=ALU.subtract,
                 op1=ALU.mult,
             )
 
-        def slope_root(first, end):
-            d = z_turned[:, 1 + first : 1 + end, :]
-            part = root[:, first:end, 0:BATCH]
+        def slope_root(first, end, bank):
             some = [P, end - first, BATCH]
-            nc.vector.tensor_mul(out=part, in0=d, in1=d)
-            nc.vector.tensor_mul(out=part, in0=part, in1=e_mv[:, first:end, 1:2].to_broadcast(some))
-            nc.vector.tensor_add(out=part, in0=part, in1=z_turned[:, 0:1, :].to_broadcast(some))
+            d = bank[:, 1 : 1 + end - first, 0:BATCH]
+            part = root[:, first:end, 0:BATCH]
+            nc.vector.tensor_mul(out=part, in0=d, in1=e_mv[:, first:end, 1:2].to_broadcast(some))
+            nc.vector.tensor_mul(out=part, in0=d, in1=part)
+            nc.vector.tensor_add(out=part, in0=bank[:, 0:1, 0:BATCH].to_broadcast(some), in1=part)
             nc.scalar.activation(out=part, in_=part, func=ACT.Sqrt)
 
-        def slope_divide(first, end):
+        def slope_divide(first, end, bank):
             part = root[:, first:end, 0:BATCH]
             nc.vector.reciprocal(out=part, in_=part)
-            nc.vector.tensor_mul(
-                out=slope[:, first:end, :], in0=part, in1=z_turned[:, 1 + first : 1 + end, :]
+            nc.vector.tensor_mul(out=slope[:, first:end, :], in0=bank[:, 1 : 1 + end - first, 0:BATCH], in1=part)
+
+        def regroup_weight(w):
+            nc.gpsimd.tensor_scalar(
+                out=w_grouped[w][:],
+                in0=w_raw[w][:].rearrange("p t n -> p n t"),
+                scalar1=1.0,
+                scalar2=0.0,
+                op0=ALU.mult,
+                op1=ALU.add,
             )
 
         def quantise_weight(w):
@@ -138,7 +148,7 @@ def tile_causalfeaturetransformer_pa_kernel(
                 out=xn[u][:],
                 in0=shaped[:, j, :],
                 scalar=slope[:, j, n : n + 1],
-                in1=be1_all[:],
+                in1=be1_bank[:],
                 op0=ALU.mult,
                 op1=ALU.add,
             )
@@ -184,31 +194,30 @@ def tile_causalfeaturetransformer_pa_kernel(
                     banks.append(acc)
             return banks
 
-        def add_bias_and_store(c, h, banks):
-            j, n = divmod(PAIR * c + h, BATCH)
-            for w in range(2):
-                b = 2 * h + w
-                res = result[2 * PAIR * c + b]
-                nc.vector.tensor_add(out=res[:], in0=banks[b][:], in1=spread[2 + w][:])
-                nc.sync.dma_start(out=outs[w][n, j * P : (j + 1) * P, :], in_=res[:])
+        def add_bias_and_store(c, b, banks):
+            j, n = divmod(PAIR * c + b // 2, BATCH)
+            res = result[PAIR_BANKS * c + b]
+            nc.vector.tensor_add(out=res[:], in0=banks[b][:], in1=bias_all[b % 2][:])
+            nc.sync.dma_start(out=outs[b % 2][n, j * P : (j + 1) * P, :], in_=res[:])
 
-        def load_vector(r, vector):
-            nc.sync.dma_start(out=vec_rows[r : r + 1, :], in_=vector.rearrange("(a k) -> a k", a=1))
+        def load_row(rows, r, vector):
+            nc.sync.dma_start(out=rows[r : r + 1, :], in_=vector.rearrange("(a k) -> a k", a=1))
 
         def load_weight(w):
             nc.sync.dma_start(out=w_raw[w][:], in_=weights[w].rearrange("(t p) n -> p t n", p=P))
 
-        nc.vector.memset(vec_rows[:], 0.0)
+        nc.vector.memset(norm_rows[:], 0.0)
+        nc.vector.memset(bias_rows[:], 0.0)
         nc.sync.dma_start(out=z_rows[0:BATCH, 0:D_FEAT], in_=Z)
         nc.sync.dma_start(out=emb[:, 0, :], in_=feat_emb[0:P, :])
-        load_vector(0, g1)
-        load_vector(1, be1)
-        load_vector(2, bk)
-        load_vector(3, bv)
+        load_row(norm_rows, 0, g1)
+        load_row(norm_rows, 1, be1)
         nc.sync.dma_start(out=emb[:, 1, :], in_=feat_emb[P : 2 * P, :])
+        nc.sync.dma_start(out=emb[:, 2, :], in_=feat_emb[2 * P : 3 * P, :])
         load_weight(0)
         load_weight(1)
-        nc.sync.dma_start(out=emb[:, 2, :], in_=feat_emb[2 * P : 3 * P, :])
+        load_row(bias_rows, 0, bk)
+        load_row(bias_rows, 1, bv)
         last = (BLOCKS - 1) * P
         nc.sync.dma_start(out=emb[0:112, BLOCKS - 1, :], in_=feat_emb[last : last + 112, :])
         nc.sync.dma_start(out=emb[112:127, BLOCKS - 1, :], in_=feat_emb[last + 112 : D_FEAT, :])
@@ -237,47 +246,39 @@ def tile_causalfeaturetransformer_pa_kernel(
             op1=ALU.mult,
         )
         nc.vector.tensor_scalar_add(out=z_var_eps[rows4, :], in0=z_mv[rows4, 1:2], scalar1=EPS)
-        spread_vector(0)
-        spread_vector(1)
+        g1_bank = spread_row(norm_rows, 0)
+        be1_bank = spread_row(norm_rows, 1)
+        nc.scalar.copy(out=be1_all[:], in_=be1_bank[:])
         nc.scalar.activation(
             out=z_terms[rows4, P + D_FEAT : P + SEQ], in_=z_var_eps[rows4, :], func=ACT.Sqrt
         )
-        measure(0)
+        regroup_weight(0)
+        regroup_weight(1)
+        early = BLOCKS - 1
+        early_bank = turn_z_terms(0, early)
+        late_bank = turn_z_terms(early, BLOCKS)
+        for j in range(early):
+            measure(j)
+        slope_root(0, early, early_bank)
         shape(0)
-        turn_z_terms(0, 2)
-        slope_root(0, 1)
-        measure(1)
-        slope_divide(0, 1)
-        spread_vector(2)
-        spread_vector(3)
-        nc.scalar.copy(out=w_grouped[0][:], in_=w_raw[0][:].rearrange("p t n -> p n t"))
-        nc.gpsimd.tensor_scalar(
-            out=w_grouped[1][:],
-            in0=w_raw[1][:].rearrange("p t n -> p n t"),
-            scalar1=1.0,
-            scalar2=0.0,
-            op0=ALU.mult,
-            op1=ALU.add,
-        )
+        shape(1)
+        slope_divide(0, early, early_bank)
+        for u in range(VECTOR_UNITS, 2 * VECTOR_UNITS):
+            form_on_scalar_and_gpsimd(u)
         form_on_vector(0)
         form_on_vector(1)
-        turn_z_terms(2, 1 + BLOCKS)
-        measure(2)
-        measure(3)
-        slope_root(1, BLOCKS)
-        shape(1)
-        slope_divide(1, BLOCKS)
-        form_on_scalar_and_gpsimd(4)
-        form_on_scalar_and_gpsimd(5)
+        measure(early)
+        slope_root(early, BLOCKS, late_bank)
         turn_and_regroup(0)
+        for w in range(2):
+            nc.scalar.copy(out=bias_all[w][:], in_=spread_row(bias_rows, w)[:])
         form_on_vector(2)
         form_on_vector(3)
-        form_on_scalar_and_gpsimd(6)
-        form_on_scalar_and_gpsimd(7)
+        shape(2)
+        slope_divide(early, BLOCKS, late_bank)
         turn_and_regroup(1)
         quantise_weight(0)
         quantise_weight(1)
-        shape(2)
         quantise(0)
         shape(3)
 
@@ -288,7 +289,7 @@ def tile_causalfeaturetransformer_pa_kernel(
                     form_on_scalar_and_gpsimd(PAIR * (step + FORM_AHEAD) + h)
             if step + TURN_AHEAD < PAIRS:
                 turn_and_regroup(step + TURN_AHEAD)
-            add_bias_and_store(step, 0, banks)
-            if step + 1 < PAIRS:
-                quantise(step + 1)
-            add_bias_and_store(step, 1, banks)
+            for b in range(PAIR_BANKS):
+                if b == 1 and step + 1 < PAIRS:
+                    quantise(step + 1)
+                add_bias_and_store(step, b, banks)

@@ -28,6 +28,7 @@ PAIR_BANKS = 2 * PAIR
 VECTOR_UNITS = BATCH
 TURN_AHEAD = 2
 FORM_AHEAD = 4
+HELP_FROM = PAIRS - FORM_AHEAD + 1
 
 FLOPS = 2 * BATCH * SEQ * D_EMB * 2 * D_OUT
 
@@ -78,6 +79,7 @@ def tile_causalfeaturetransformer_pa_kernel(
         x_codes = [keep.tile([P, PAIR * P], U32, name="x_codes%d" % c, align_bytes=64) for c in range(PAIRS)]
         x_scales = [keep.tile([P, PAIR * P], U8, name="x_scales%d" % c, align_bytes=64) for c in range(PAIRS)]
         result = [keep.tile([P, D_OUT], F32, name="result%d" % b) for b in range(2 * UNITS)]
+        unbiased = {c: keep.tile([P, D_OUT], F32, name="unbiased%d" % c) for c in range(HELP_FROM, PAIRS)}
 
         def spread_row(rows, r):
             bank = acc_banks.tile([P, D_EMB], F32, name="acc")
@@ -194,11 +196,18 @@ def tile_causalfeaturetransformer_pa_kernel(
                     banks.append(acc)
             return banks
 
-        def add_bias_and_store(c, b, banks):
+        def add_bias_on_vector(c, b, banks):
+            nc.vector.tensor_add(out=result[PAIR_BANKS * c + b][:], in0=banks[b][:], in1=bias_all[b % 2][:])
+
+        def add_bias_on_scalar_and_gpsimd(c, b, banks):
+            nc.scalar.copy(out=unbiased[c][:], in_=banks[b][:])
+            nc.gpsimd.tensor_tensor(
+                out=result[PAIR_BANKS * c + b][:], in0=unbiased[c][:], in1=bias_all[b % 2][:], op=ALU.add
+            )
+
+        def store(c, b):
             j, n = divmod(PAIR * c + b // 2, BATCH)
-            res = result[PAIR_BANKS * c + b]
-            nc.vector.tensor_add(out=res[:], in0=banks[b][:], in1=bias_all[b % 2][:])
-            nc.sync.dma_start(out=outs[b % 2][n, j * P : (j + 1) * P, :], in_=res[:])
+            nc.sync.dma_start(out=outs[b % 2][n, j * P : (j + 1) * P, :], in_=result[PAIR_BANKS * c + b][:])
 
         def load_row(rows, r, vector):
             nc.sync.dma_start(out=rows[r : r + 1, :], in_=vector.rearrange("(a k) -> a k", a=1))
@@ -254,7 +263,7 @@ def tile_causalfeaturetransformer_pa_kernel(
         )
         regroup_weight(0)
         regroup_weight(1)
-        early = BLOCKS - 1
+        early = BLOCKS // 2
         early_bank = turn_z_terms(0, early)
         late_bank = turn_z_terms(early, BLOCKS)
         for j in range(early):
@@ -267,7 +276,8 @@ def tile_causalfeaturetransformer_pa_kernel(
             form_on_scalar_and_gpsimd(u)
         form_on_vector(0)
         form_on_vector(1)
-        measure(early)
+        for j in range(early, BLOCKS):
+            measure(j)
         slope_root(early, BLOCKS, late_bank)
         turn_and_regroup(0)
         for w in range(2):
@@ -287,9 +297,15 @@ def tile_causalfeaturetransformer_pa_kernel(
             if step + FORM_AHEAD < PAIRS:
                 for h in range(PAIR):
                     form_on_scalar_and_gpsimd(PAIR * (step + FORM_AHEAD) + h)
+            helped = step >= HELP_FROM
+            if helped:
+                add_bias_on_scalar_and_gpsimd(step, 0, banks)
             if step + TURN_AHEAD < PAIRS:
                 turn_and_regroup(step + TURN_AHEAD)
-            for b in range(PAIR_BANKS):
+            for b in range(1 if helped else 0, PAIR_BANKS):
                 if b == 1 and step + 1 < PAIRS:
                     quantise(step + 1)
-                add_bias_and_store(step, b, banks)
+                add_bias_on_vector(step, b, banks)
+                store(step, b)
+                if helped and b == PAIR_BANKS // 2:
+                    store(step, 0)

from contextlib import ExitStack

import concourse.mybir as mybir
from concourse.masks import make_identity

F32 = mybir.dt.float32
BF16 = mybir.dt.bfloat16
U32 = mybir.dt.uint32
U8 = mybir.dt.uint8
FP8X4 = mybir.dt.float8_e4m3fn_x4
ALU = mybir.AluOpType
ACT = mybir.ActivationFunctionType

P = 128
PACK = 4
BATCH = 4
D_FEAT = 511
SEQ = D_FEAT + 1
D_EMB = 512
D_OUT = 512
BLOCKS = SEQ // P
EPS = 1e-5

UNITS = BLOCKS * BATCH
PAIR = 2
PAIRS = UNITS // PAIR
PAIR_BANKS = 2 * PAIR
VECTOR_UNITS = BATCH
TURN_AHEAD = 2
FORM_AHEAD = 4
HELP_FROM = PAIRS - FORM_AHEAD + 1

FLOPS = 2 * BATCH * SEQ * D_EMB * 2 * D_OUT


def tile_causalfeaturetransformer_pa_kernel(
    tc, Z, feat_emb, label_token, g1, be1, wk, bk, wv, bv, out_0, out_1
):
    nc = tc.nc
    weights = (wk, wv)
    outs = (out_0, out_1)

    with ExitStack() as ctx:
        keep = ctx.enter_context(tc.tile_pool(name="keep", bufs=1))
        turned_banks = ctx.enter_context(tc.psum_pool(name="turned_banks", bufs=2))
        acc_banks = ctx.enter_context(tc.psum_pool(name="acc_banks", bufs=6))
        ctx.enter_context(tc.manual_schedule())

        ident = keep.tile([P, P], F32)
        ident_bf = keep.tile([P, P], BF16)
        warm = keep.tile([P, 1], F32)
        z_rows = keep.tile([P, SEQ], BF16)
        norm_rows = keep.tile([P, D_EMB], BF16)
        bias_rows = keep.tile([P, D_OUT], BF16)
        emb = keep.tile([P, BLOCKS, D_EMB], BF16)
        z_stats = keep.tile([P, 6], F32)
        z_mv = keep.tile([P, 2], F32)
        z_var_eps = keep.tile([P, 1], F32)
        z_terms = keep.tile([P, P + SEQ], F32)
        e_stats = keep.tile([P, BLOCKS, 6], F32)
        e_mv = keep.tile([P, BLOCKS, 2], F32)
        shaped = keep.tile([P, BLOCKS, D_EMB], F32)
        root = keep.tile([P, BLOCKS, 2 * BATCH], F32)
        slope = keep.tile([P, BLOCKS, BATCH], F32)
        be1_all = keep.tile([P, D_EMB], BF16)
        bias_all = [keep.tile([P, D_OUT], BF16, name="bias_all%d" % w) for w in range(2)]
        w_raw = [keep.tile([P, PACK, D_OUT], BF16, name="w_raw%d" % w) for w in range(2)]
        w_grouped = [
            keep.tile([P, D_OUT, PACK], BF16, name="w_grouped%d" % w, align_bytes=64) for w in range(2)
        ]
        w_codes = [keep.tile([P, D_OUT], U32, name="w_codes%d" % w, align_bytes=64) for w in range(2)]
        w_scales = [keep.tile([P, D_OUT], U8, name="w_scales%d" % w, align_bytes=64) for w in range(2)]
        scaled = {u: keep.tile([P, D_EMB], F32, name="scaled%d" % u) for u in range(VECTOR_UNITS, UNITS)}
        xn = [keep.tile([P, D_EMB], BF16, name="xn%d" % u) for u in range(UNITS)]
        x_grouped = [
            keep.tile([P, PAIR, P, PACK], BF16, name="x_grouped%d" % c, align_bytes=64)
            for c in range(PAIRS)
        ]
        x_codes = [keep.tile([P, PAIR * P], U32, name="x_codes%d" % c, align_bytes=64) for c in range(PAIRS)]
        x_scales = [keep.tile([P, PAIR * P], U8, name="x_scales%d" % c, align_bytes=64) for c in range(PAIRS)]
        result = [keep.tile([P, D_OUT], F32, name="result%d" % b) for b in range(2 * UNITS)]
        unbiased = {c: keep.tile([P, D_OUT], F32, name="unbiased%d" % c) for c in range(HELP_FROM, PAIRS)}

        def spread_row(rows, r):
            bank = acc_banks.tile([P, D_EMB], F32, name="acc")
            nc.tensor.matmul(
                out=bank[:],
                lhsT=ident_bf[:, r : r + 1].to_broadcast([P, P]),
                rhs=rows[:],
                start=True,
                stop=True,
            )
            return bank

        def turn_z_terms(first, end):
            bank = turned_banks.tile([P, BLOCKS, P], F32, name="turned")
            nc.tensor.transpose(bank[:, 0, :], z_terms[:, 0:P], ident[:])
            for j in range(first, end):
                nc.tensor.transpose(bank[:, 1 + j - first, :], z_terms[:, (1 + j) * P : (2 + j) * P], ident[:])
            return bank

        def measure(j):
            nc.vector.bn_stats(out=e_stats[:, j, :], in_=emb[:, j, :])
            nc.vector.bn_aggr(out=e_mv[:, j, :], in_=e_stats[:, j, :])

        def shape(j):
            nc.vector.scalar_tensor_tensor(
                out=shaped[:, j, :],
                in0=emb[:, j, :],
                scalar=e_mv[:, j, 0:1],
                in1=g1_bank[:],
                op0=ALU.subtract,
                op1=ALU.mult,
            )

        def slope_root(first, end, bank):
            some = [P, end - first, BATCH]
            d = bank[:, 1 : 1 + end - first, 0:BATCH]
            part = root[:, first:end, 0:BATCH]
            nc.vector.tensor_mul(out=part, in0=d, in1=e_mv[:, first:end, 1:2].to_broadcast(some))
            nc.vector.tensor_mul(out=part, in0=d, in1=part)
            nc.vector.tensor_add(out=part, in0=bank[:, 0:1, 0:BATCH].to_broadcast(some), in1=part)
            nc.scalar.activation(out=part, in_=part, func=ACT.Sqrt)

        def slope_divide(first, end, bank):
            part = root[:, first:end, 0:BATCH]
            nc.vector.reciprocal(out=part, in_=part)
            nc.vector.tensor_mul(out=slope[:, first:end, :], in0=bank[:, 1 : 1 + end - first, 0:BATCH], in1=part)

        def regroup_weight(w):
            nc.gpsimd.tensor_scalar(
                out=w_grouped[w][:],
                in0=w_raw[w][:].rearrange("p t n -> p n t"),
                scalar1=1.0,
                scalar2=0.0,
                op0=ALU.mult,
                op1=ALU.add,
            )

        def quantise_weight(w):
            nc.vector.quantize_mx(
                out=w_codes[w][:].bitcast(FP8X4),
                scales=w_scales[w][:],
                in_=w_grouped[w][:].rearrange("p n t -> p (n t)"),
            )

        def form_on_vector(u):
            j, n = divmod(u, BATCH)
            nc.vector.scalar_tensor_tensor(
                out=xn[u][:],
                in0=shaped[:, j, :],
                scalar=slope[:, j, n : n + 1],
                in1=be1_bank[:],
                op0=ALU.mult,
                op1=ALU.add,
            )

        def form_on_scalar_and_gpsimd(u):
            j, n = divmod(u, BATCH)
            nc.scalar.activation(
                out=scaled[u][:], in_=shaped[:, j, :], func=ACT.Copy, scale=slope[:, j, n : n + 1]
            )
            nc.gpsimd.tensor_tensor(out=xn[u][:], in0=scaled[u][:], in1=be1_all[:], op=ALU.add)

        def turn_and_regroup(c):
            turned = turned_banks.tile([P, PAIR, PACK, P], BF16)
            for h in range(PAIR):
                for t in range(PACK):
                    nc.tensor.transpose(
                        turned[:, h, t, :], xn[PAIR * c + h][:, t * P : (t + 1) * P], ident_bf[:]
                    )
            nc.scalar.copy(out=x_grouped[c][:], in_=turned[:].rearrange("p h t r -> p h r t"))

        def quantise(c):
            nc.vector.quantize_mx(
                out=x_codes[c][:].bitcast(FP8X4),
                scales=x_scales[c][:],
                in_=x_grouped[c][:].rearrange("p h r t -> p (h r t)"),
            )

        def multiply(c):
            banks = []
            for h in range(PAIR):
                tokens = slice(h * P, (h + 1) * P)
                for w in range(2):
                    acc = acc_banks.tile([P, D_OUT], F32)
                    nc.tensor.matmul_mx(
                        out=acc[:],
                        lhsT=x_codes[c][:, tokens].bitcast(FP8X4),
                        lhsT_scale=x_scales[c][:, tokens],
                        rhs=w_codes[w][:].bitcast(FP8X4),
                        rhs_scale=w_scales[w][:],
                        start=True,
                        stop=True,
                    )
                    banks.append(acc)
            return banks

        def add_bias_on_vector(c, b, banks):
            nc.vector.tensor_add(out=result[PAIR_BANKS * c + b][:], in0=banks[b][:], in1=bias_all[b % 2][:])

        def add_bias_on_scalar_and_gpsimd(c, b, banks):
            nc.scalar.copy(out=unbiased[c][:], in_=banks[b][:])
            nc.gpsimd.tensor_tensor(
                out=result[PAIR_BANKS * c + b][:], in0=unbiased[c][:], in1=bias_all[b % 2][:], op=ALU.add
            )

        def store(c, b):
            j, n = divmod(PAIR * c + b // 2, BATCH)
            nc.sync.dma_start(out=outs[b % 2][n, j * P : (j + 1) * P, :], in_=result[PAIR_BANKS * c + b][:])

        def load_row(rows, r, vector):
            nc.sync.dma_start(out=rows[r : r + 1, :], in_=vector.rearrange("(a k) -> a k", a=1))

        def load_weight(w):
            nc.sync.dma_start(out=w_raw[w][:], in_=weights[w].rearrange("(t p) n -> p t n", p=P))

        nc.vector.memset(norm_rows[:], 0.0)
        nc.vector.memset(bias_rows[:], 0.0)
        nc.sync.dma_start(out=z_rows[0:BATCH, 0:D_FEAT], in_=Z)
        nc.sync.dma_start(out=emb[:, 0, :], in_=feat_emb[0:P, :])
        load_row(norm_rows, 0, g1)
        load_row(norm_rows, 1, be1)
        nc.sync.dma_start(out=emb[:, 1, :], in_=feat_emb[P : 2 * P, :])
        nc.sync.dma_start(out=emb[:, 2, :], in_=feat_emb[2 * P : 3 * P, :])
        load_weight(0)
        load_weight(1)
        load_row(bias_rows, 0, bk)
        load_row(bias_rows, 1, bv)
        last = (BLOCKS - 1) * P
        nc.sync.dma_start(out=emb[0:112, BLOCKS - 1, :], in_=feat_emb[last : last + 112, :])
        nc.sync.dma_start(out=emb[112:127, BLOCKS - 1, :], in_=feat_emb[last + 112 : D_FEAT, :])
        nc.sync.dma_start(
            out=emb[127:128, BLOCKS - 1, :], in_=label_token.rearrange("a b k -> (a b) k")
        )

        make_identity(nc, ident[:])
        nc.gpsimd.memset(z_terms[:], 0.0)
        nc.vector.memset(warm[:], 1.0)
        nc.scalar.activation(out=warm[:], in_=warm[:], func=ACT.Sqrt)
        nc.vector.tensor_copy(out=ident_bf[:], in_=ident[:])

        rows4 = slice(0, BATCH)
        nc.vector.bn_stats(out=z_stats[rows4, :], in_=z_rows[rows4, 0:D_FEAT])
        nc.vector.bn_aggr(out=z_mv[rows4, :], in_=z_stats[rows4, :])
        nc.vector.tensor_scalar_sub(
            out=z_terms[rows4, P : P + D_FEAT], in0=z_rows[rows4, 0:D_FEAT], scalar1=z_mv[rows4, 0:1]
        )
        nc.vector.tensor_scalar(
            out=z_terms[rows4, 0:P],
            in0=z_mv[rows4, 1:2].to_broadcast([BATCH, P]),
            scalar1=EPS,
            scalar2=EPS,
            op0=ALU.add,
            op1=ALU.mult,
        )
        nc.vector.tensor_scalar_add(out=z_var_eps[rows4, :], in0=z_mv[rows4, 1:2], scalar1=EPS)
        g1_bank = spread_row(norm_rows, 0)
        be1_bank = spread_row(norm_rows, 1)
        nc.scalar.copy(out=be1_all[:], in_=be1_bank[:])
        nc.scalar.activation(
            out=z_terms[rows4, P + D_FEAT : P + SEQ], in_=z_var_eps[rows4, :], func=ACT.Sqrt
        )
        regroup_weight(0)
        regroup_weight(1)
        early = BLOCKS // 2
        early_bank = turn_z_terms(0, early)
        late_bank = turn_z_terms(early, BLOCKS)
        for j in range(early):
            measure(j)
        slope_root(0, early, early_bank)
        shape(0)
        shape(1)
        slope_divide(0, early, early_bank)
        for u in range(VECTOR_UNITS, 2 * VECTOR_UNITS):
            form_on_scalar_and_gpsimd(u)
        form_on_vector(0)
        form_on_vector(1)
        for j in range(early, BLOCKS):
            measure(j)
        slope_root(early, BLOCKS, late_bank)
        turn_and_regroup(0)
        for w in range(2):
            nc.scalar.copy(out=bias_all[w][:], in_=spread_row(bias_rows, w)[:])
        form_on_vector(2)
        form_on_vector(3)
        shape(2)
        slope_divide(early, BLOCKS, late_bank)
        turn_and_regroup(1)
        quantise_weight(0)
        quantise_weight(1)
        quantise(0)
        shape(3)

        for step in range(PAIRS):
            banks = multiply(step)
            if step + FORM_AHEAD < PAIRS:
                for h in range(PAIR):
                    form_on_scalar_and_gpsimd(PAIR * (step + FORM_AHEAD) + h)
            helped = step >= HELP_FROM
            if helped:
                add_bias_on_scalar_and_gpsimd(step, 0, banks)
            if step + TURN_AHEAD < PAIRS:
                turn_and_regroup(step + TURN_AHEAD)
            for b in range(1 if helped else 0, PAIR_BANKS):
                if b == 1 and step + 1 < PAIRS:
                    quantise(step + 1)
                add_bias_on_vector(step, b, banks)
                store(step, b)
                if helped and b == PAIR_BANKS // 2:
                    store(step, 0)
